import numpy as np
import ml_dtypes


def mxq(x, axis, fmt="e4m3"):
    dtype, down = {"e4m3": (ml_dtypes.float8_e4m3fn, 7), "e5m2": (ml_dtypes.float8_e5m2, 14)}[fmt]
    v = np.moveaxis(np.asarray(x, np.float32).astype(ml_dtypes.bfloat16).astype(np.float64), axis, -1)
    blocks = v.reshape(v.shape[:-1] + (-1, 32))
    amax = np.abs(blocks).max(-1, keepdims=True)
    byte = np.maximum(np.where(amax > 0, np.frexp(amax)[1] - 1 + 127, 0) - down, 1)
    scale = np.exp2(byte - 127.0)
    codes = (blocks / scale).astype(np.float32).astype(dtype).astype(np.float64)
    return np.moveaxis((codes * scale).reshape(v.shape), -1, axis)


WIDE = False


def mx_kscale(k):
    if not WIDE:
        return np.ones(k)
    levels = np.array([10, -10, 5, -5, 0])
    a = np.random.permutation(np.resize(levels, k // 512 * 4)).reshape(k // 512, 4)
    idx = np.arange(k)
    return np.exp2(a[idx // 512, idx % 128 // 32])


BF16 = ml_dtypes.bfloat16


def bf(x):
    return np.asarray(x, np.float32).astype(BF16)


def f64(x):
    return np.asarray(x).astype(np.float64)


B, C, H, W, K, HID, LAT = 4, 512, 16, 16, 8, 512, 32
REDUCTION = -0.1
CLAMP = 500.0
HOT = 1.2 * CLAMP / (-REDUCTION * C * np.sqrt(2.0 / np.pi))


def setup_inputs():
    s = mx_kscale(HID)
    amp = np.where(np.random.random((B, 1, H, W)) < 0.125, HOT, 1.0)
    return {"d": bf(np.tanh(np.random.standard_normal((K, B, HID, H, W))) * s[:, None, None]),
            "W_dec": bf(np.random.standard_normal((K, C, HID)) * 1.1 / np.sqrt(HID) / s),
            "x": bf(np.random.standard_normal((B, C, H, W)) * amp)}


def reference(d, W_dec, x):
    xf = f64(x)
    wq = mxq(f64(W_dec), 2, "e4m3")
    dq = mxq(f64(d), 2, "e4m3")
    recon = (wq[:, None] @ dq.reshape(K, B, HID, H * W)).reshape(K, B, C, H, W)
    err = np.sum(np.abs(recon - xf[None]), axis=2) * REDUCTION
    logits = np.swapaxes(np.clip(err, -CLAMP, CLAMP), 0, 1)
    e = np.exp(logits - logits.max(axis=1, keepdims=True))
    p = e / e.sum(axis=1, keepdims=True)
    error = np.mean(logits, axis=(2, 3))
    return p, error, np.swapaxes(recon, 0, 1)

@@ -1,0 +1,316 @@
+from contextlib import ExitStack
+
+import concourse.mybir as mybir
+from concourse.masks import make_identity
+
+FP8X4 = mybir.dt.float8_e4m3fn_x4
+BF16 = mybir.dt.bfloat16
+F32 = mybir.dt.float32
+U32 = mybir.dt.uint32
+U8 = mybir.dt.uint8
+ALU = mybir.AluOpType
+ACT = mybir.ActivationFunctionType
+AX = mybir.AxisListType
+
+P = 128
+NK, NB, NC, NJ, NW = 8, 4, 512, 512, 256
+FLOPS = 2 * NK * NB * NC * NJ * NW
+
+MANUAL = False
+STORE_Q = "gpsimd"
+LEAD = 4
+
+
+def tile_cssrclassifier_pa_kernel(tc, d, W_dec, x, out_0, out_1, out_2):
+    nc = tc.nc
+    with ExitStack() as ctx:
+        const = ctx.enter_context(tc.tile_pool(name="const", bufs=1))
+        raw = ctx.enter_context(tc.tile_pool(name="raw", bufs=NK))
+        grp = ctx.enter_context(tc.tile_pool(name="grp", bufs=2))
+        mx = ctx.enter_context(tc.tile_pool(name="mx", bufs=3))
+        recp = ctx.enter_context(tc.tile_pool(name="recp", bufs=4))
+        junk = ctx.enter_context(tc.tile_pool(name="junk", bufs=2))
+        ps_a = ctx.enter_context(tc.psum_pool(name="ps_a", bufs=2))
+        ps_b = ctx.enter_context(tc.psum_pool(name="ps_b", bufs=3))
+        aux = ctx.enter_context(tc.psum_pool(name="aux", bufs=3))
+        if MANUAL:
+            ctx.enter_context(tc.manual_schedule())
+
+        store_eng = {"gpsimd": nc.gpsimd, "scalar": nc.scalar, "sync": nc.sync}[STORE_Q]
+
+        warm = const.tile([P, 1], F32)
+        nc.vector.memset(warm[:], 0.0)
+        warm2 = const.tile([P, 1], F32)
+        nc.scalar.activation(out=warm2[:], in_=warm[:], func=ACT.Exp)
+        ident_f = const.tile([P, P], F32)
+        make_identity(nc, ident_f[:])
+        ident_b = const.tile([P, P], BF16)
+        make_identity(nc, ident_b[:])
+        ones_f = const.tile([P, P], F32)
+        nc.vector.memset(ones_f[:], 1.0 / NW)
+        pad = const.tile([P, P], F32)
+        nc.vector.memset(pad[:], 0.0)
+
+        smax = const.tile([P, 64], F32)
+        sr = const.tile([P, 64], F32)
+        sx = const.tile([P, 8], F32)
+        x_sb = const.tile([P, NB, 4, NW], BF16)
+        x_t = const.tile([P, 8, NC], BF16)
+
+        w_raw = []
+        d_raw = []
+        for k in range(NK):
+            wr = raw.tile([P, 4, NJ], BF16, name="w_raw%d" % k, tag="w_raw")
+            nc.sync.dma_start(out=wr[:], in_=W_dec[k].rearrange("(p t) j -> p t j", t=4))
+            w_raw.append(wr)
+            dr = raw.tile([P, NB, 4, NW], BF16, name="d_raw%d" % k, tag="d_raw")
+            dst = dr[:].rearrange("q b (u e) w -> q (b u) (e w)", u=2)
+            if k == 0:
+                for bp in range(2):
+                    nc.sync.dma_start(
+                        out=dst[:, 4 * bp : 4 * bp + 4, :],
+                        in_=d[k, 2 * bp : 2 * bp + 2].rearrange("b (u q e) h w -> q (b u) (e h w)", u=2, q=P, e=2),
+                    )
+                nc.sync.dma_start(
+                    out=x_sb[:].rearrange("p b t w -> p b (t w)"),
+                    in_=x.rearrange("b (p t) h w -> p b (t h w)", t=4),
+                )
+            else:
+                nc.sync.dma_start(out=dst, in_=d[k].rearrange("b (u q e) h w -> q (b u) (e h w)", u=2, q=P, e=2))
+            d_raw.append(dr)
+
+        state = {}
+
+        def w_transposes(k):
+            wf = w_raw[k][:].bitcast(F32)
+            banks = []
+            for g in range(2):
+                wt = aux.tile([P, 4, P], F32, name="wt%d_%d" % (k, g), tag="aux")
+                for tt in range(2):
+                    for u in range(2):
+                        nc.tensor.transpose(wt[:, tt * 2 + u, :], wf[:, 2 * g + tt, u * P : (u + 1) * P], ident_f[:])
+                banks.append(wt)
+            wg = grp.tile([P, NC, 4], BF16, name="wg%d" % k, tag="wg", align_bytes=64)
+            wgf = wg[:].bitcast(F32)
+            for g in range(2):
+                nc.scalar.copy(
+                    out=wgf[:, g * 256 : (g + 1) * 256, :].rearrange("q (tt p) u -> q tt p u", tt=2),
+                    in_=banks[g][:].rearrange("q (tt u) p -> q tt p u", u=2),
+                )
+            state[("wg", k)] = wg
+
+        def q_w(k):
+            wg = state[("wg", k)]
+            wc = mx.tile([P, NC], U32, name="wc%d" % k, tag="wc", align_bytes=64)
+            ws = mx.tile([P, NC], U8, name="ws%d" % k, tag="ws", align_bytes=64)
+            nc.vector.quantize_mx(out=wc[:].bitcast(FP8X4), scales=ws[:], in_=wg[:].rearrange("q c t -> q (c t)"))
+            state[("wc", k)] = wc
+            state[("ws", k)] = ws
+
+        def d_views(k):
+            if ("dg", k) not in state:
+                dg = grp.tile([P, NB, NW, 4], BF16, name="dg%d" % k, tag="dg", align_bytes=64)
+                state[("dg", k)] = dg
+            dg = state[("dg", k)]
+            src = d_raw[k][:].rearrange("q b t (c i) -> q b c t i", i=4)
+            dst = dg[:].rearrange("q b (c i) t -> q b c t i", i=4)
+            return src, dst
+
+        def rg_v01(k):
+            src, dst = d_views(k)
+            nc.vector.tensor_copy(out=dst[:, 0:2], in_=src[:, 0:2])
+
+        def rg_v2(k):
+            src, dst = d_views(k)
+            nc.vector.tensor_copy(out=dst[:, 2], in_=src[:, 2])
+
+        def rg_s3(k):
+            src, dst = d_views(k)
+            nc.scalar.copy(out=dst[:, 3], in_=src[:, 3])
+
+        def q_d(k, bp):
+            if ("dc", k) not in state:
+                dc_new = mx.tile([P, NB * NW], U32, name="dc%d" % k, tag="dc", align_bytes=64)
+                ds_new = mx.tile([P, NB * NW], U8, name="ds%d" % k, tag="ds", align_bytes=64)
+                state[("dc", k)] = dc_new
+                state[("ds", k)] = ds_new
+            dc = state[("dc", k)]
+            ds = state[("ds", k)]
+            dg = state[("dg", k)]
+            cols = slice(bp * 512, (bp + 1) * 512)
+            nc.vector.quantize_mx(
+                out=dc[:, cols].bitcast(FP8X4),
+                scales=ds[:, cols],
+                in_=dg[:, 2 * bp : 2 * bp + 2].rearrange("q b w t -> q (b w t)"),
+            )
+
+        def x_path():
+            for i in range(8):
+                b, h = divmod(i, 2)
+                xp = aux.tile([P, NC], BF16, name="xp%d" % i, tag="aux")
+                for t in range(4):
+                    nc.tensor.transpose(xp[:, t * P : (t + 1) * P], x_sb[:, b, t, h * P : (h + 1) * P], ident_b[:])
+                nc.scalar.activation(out=x_t[:, i, :], in_=xp[:], func=ACT.Copy, accum_out=sx[:, i : i + 1])
+
+        def path_a(k, i):
+            bp, t = divmod(i, 4)
+            wc, ws, dc, ds = state[("wc", k)], state[("ws", k)], state[("dc", k)], state[("ds", k)]
+            if t == 0:
+                rec_new = recp.tile([P, 2, 4, NW], F32, name="rec%d_%d" % (k, bp), tag="rec")
+                state["rec"] = rec_new
+            rec = state["rec"]
+            pa = ps_a.tile([P, 512], F32, name="pa%d_%d" % (k, i), tag="pa")
+            mc = slice(t * P, (t + 1) * P)
+            ncol = slice(bp * 512, (bp + 1) * 512)
+            nc.tensor.matmul_mx(
+                out=pa[:],
+                lhsT=wc[:, mc].bitcast(FP8X4),
+                lhsT_scale=ws[:, mc],
+                rhs=dc[:, ncol].bitcast(FP8X4),
+                rhs_scale=ds[:, ncol],
+                start=True,
+                stop=True,
+            )
+            nc.scalar.copy(out=rec[:, :, t, :], in_=pa[:].rearrange("p (b w) -> p b w", b=2))
+            if t == 3:
+                store_eng.dma_start(
+                    out=out_2[2 * bp : 2 * bp + 2, k].rearrange("b (p t) h w -> p b (t h w)", t=4),
+                    in_=rec[:].rearrange("p b t w -> p b (t w)"),
+                )
+
+        def path_b(k, i):
+            b, h = divmod(i, 2)
+            wc, ws, dc, ds = state[("wc", k)], state[("ws", k)], state[("dc", k)], state[("ds", k)]
+            mc = slice(i * P, (i + 1) * P)
+            col = b * 16 + k * 2 + h
+            pb = ps_b.tile([P, 512], F32, name="pb%d_%d" % (k, i), tag="pb")
+            nc.tensor.matmul_mx(
+                out=pb[:],
+                lhsT=dc[:, mc].bitcast(FP8X4),
+                lhsT_scale=ds[:, mc],
+                rhs=wc[:].bitcast(FP8X4),
+                rhs_scale=ws[:],
+                start=True,
+                stop=True,
+            )
+            g = i % 4
+            if g == 0:
+                pc_new = aux.tile([P, 4, P], F32, name="pc%d_%d" % (k, i), tag="aux")
+                state["pc"] = pc_new
+            pc = state["pc"]
+            for t in range(4):
+                tc_ = slice(t * P, (t + 1) * P)
+                nc.tensor.matmul_mx(
+                    out=pc[:, g, :],
+                    lhsT=dc[:, mc].bitcast(FP8X4),
+                    lhsT_scale=ds[:, mc],
+                    rhs=wc[:, tc_].bitcast(FP8X4),
+                    rhs_scale=ws[:, tc_],
+                    start=(t == 0),
+                    stop=(t == 3),
+                )
+            jk = junk.tile([P, 512], BF16, name="jk%d_%d" % (k, i), tag="jk")
+            nc.vector.scalar_tensor_tensor(
+                out=jk[:],
+                in0=pb[:],
+                scalar=1.0,
+                in1=x_t[:, i, :],
+                op0=ALU.mult,
+                op1=ALU.max,
+                accum_out=smax[:, col : col + 1],
+            )
+            if g == 3:
+                for gg in range(4):
+                    ii = i - 3 + gg
+                    cc = (ii // 2) * 16 + k * 2 + (ii % 2)
+                    jc = junk.tile([P, P], BF16, name="jc%d_%d" % (k, ii), tag="jc")
+                    nc.scalar.activation(out=jc[:], in_=pc[:, gg, :], func=ACT.Copy, accum_out=sr[:, cc : cc + 1])
+
+        w_transposes(0)
+        rg_v01(0)
+        rg_v2(0)
+        rg_s3(0)
+        q_w(0)
+        q_d(0, 0)
+        q_d(0, 1)
+
+        total = NK * 8
+        for s in range(total + LEAD):
+            if s < total:
+                path_a(s // 8, s % 8)
+            if s == LEAD - 1:
+                x_path()
+            if s >= LEAD:
+                path_b((s - LEAD) // 8, (s - LEAD) % 8)
+            k, i = divmod(s, 8)
+            if k + 1 < NK:
+                if i == 0:
+                    rg_v01(k + 1)
+                elif i == 1:
+                    w_transposes(k + 1)
+                elif i == 2:
+                    rg_v2(k + 1)
+                    rg_s3(k + 1)
+                elif i == 4:
+                    q_w(k + 1)
+                elif i == 5:
+                    q_d(k + 1, 0)
+                elif i == 7:
+                    q_d(k + 1, 1)
+
+        def v4(ap):
+            return ap.rearrange("p (b k h) -> p b k h", b=NB, k=NK, h=2)
+
+        def bc(ap):
+            return ap.rearrange("p (b h) -> p b h", h=2).unsqueeze(2).to_broadcast([P, NB, NK, 2])
+
+        t1 = const.tile([P, 64], F32)
+        nc.vector.scalar_tensor_tensor(out=t1[:], in0=smax[:], scalar=2.0, in1=sr[:], op0=ALU.mult, op1=ALU.subtract)
+        t2 = const.tile([P, 64], F32)
+        nc.vector.tensor_tensor(out=v4(t2[:]), in0=v4(t1[:]), in1=bc(sx[:]), op=ALU.subtract)
+        lg0 = const.tile([P, 64], F32)
+        nc.vector.tensor_scalar(out=lg0[:], in0=t2[:], scalar1=-0.1, scalar2=-500.0, op0=ALU.mult, op1=ALU.max)
+        lg = const.tile([P, 64], F32)
+        nc.vector.tensor_scalar_min(out=lg[:], in0=lg0[:], scalar1=500.0)
+        mxk = const.tile([P, 8], F32)
+        nc.vector.tensor_reduce(
+            out=mxk[:].rearrange("p (b h) -> p b h", h=2),
+            in_=lg[:].rearrange("p (b k h) -> p b h k", b=NB, k=NK, h=2),
+            axis=AX.X,
+            op=ALU.max,
+        )
+        sh = const.tile([P, 64], F32)
+        nc.vector.tensor_tensor(out=v4(sh[:]), in0=v4(lg[:]), in1=bc(mxk[:]), op=ALU.subtract)
+        ex = const.tile([P, 64], F32)
+        nc.scalar.activation(out=ex[:], in_=sh[:], func=ACT.Exp)
+        den = const.tile([P, 8], F32)
+        nc.vector.tensor_reduce(
+            out=den[:].rearrange("p (b h) -> p b h", h=2),
+            in_=ex[:].rearrange("p (b k h) -> p b h k", b=NB, k=NK, h=2),
+            axis=AX.X,
+            op=ALU.add,
+        )
+        rden = const.tile([P, 8], F32)
+        nc.vector.reciprocal(out=rden[:], in_=den[:])
+        nc.vector.tensor_tensor(out=v4(pad[:, 0:64]), in0=v4(ex[:]), in1=bc(rden[:]), op=ALU.mult)
+        pt = aux.tile([P, P], F32, name="pt", tag="aux")
+        nc.tensor.transpose(pt[:], pad[:], ident_f[:])
+        p_out = const.tile([P, P], F32)
+        nc.vector.tensor_copy(out=p_out[:], in_=pt[:])
+        nc.sync.dma_start(out=out_0.rearrange("b k (h r) w -> (b k h) (r w)", h=2), in_=p_out[0:64, :])
+
+        lsum = const.tile([P, 32], F32)
+        lg3 = lg[:].rearrange("p (c h) -> p c h", h=2)
+        nc.vector.tensor_tensor(out=lsum[:], in0=lg3[:, :, 0], in1=lg3[:, :, 1], op=ALU.add)
+        pe_ = aux.tile([P, 32], F32, name="pe_", tag="aux")
+        nc.tensor.matmul(out=pe_[:], lhsT=ones_f[:], rhs=lsum[:], start=True, stop=True)
+        e_sel = const.tile([P, NB, NK], F32)
+        nc.vector.tensor_tensor(
+            out=e_sel[:],
+            in0=pe_[:].rearrange("p (b k) -> p b k", b=NB),
+            in1=ident_f[:, 0:NB].unsqueeze(2).to_broadcast([P, NB, NK]),
+            op=ALU.mult,
+        )
+        e_out = const.tile([P, NK], F32)
+        nc.vector.tensor_reduce(out=e_out[:], in_=e_sel[:].rearrange("p b k -> p k b"), axis=AX.X, op=ALU.add)
+        nc.sync.dma_start(out=out_1, in_=e_out[0:NB, :])

@@ -16,9 +16,7 @@ P = 128
 NK, NB, NC, NJ, NW = 8, 4, 512, 512, 256
 FLOPS = 2 * NK * NB * NC * NJ * NW
 
-MANUAL = False
-STORE_Q = "gpsimd"
-LEAD = 4
+MANUAL = True
 
 
 def tile_cssrclassifier_pa_kernel(tc, d, W_dec, x, out_0, out_1, out_2):
@@ -36,8 +34,6 @@ def tile_cssrclassifier_pa_kernel(tc, d, W_dec, x, out_0, out_1, out_2):
         if MANUAL:
             ctx.enter_context(tc.manual_schedule())
 
-        store_eng = {"gpsimd": nc.gpsimd, "scalar": nc.scalar, "sync": nc.sync}[STORE_Q]
-
         warm = const.tile([P, 1], F32)
         nc.vector.memset(warm[:], 0.0)
         warm2 = const.tile([P, 1], F32)
@@ -52,52 +48,63 @@ def tile_cssrclassifier_pa_kernel(tc, d, W_dec, x, out_0, out_1, out_2):
         nc.vector.memset(pad[:], 0.0)
 
         smax = const.tile([P, 64], F32)
-        sr = const.tile([P, 64], F32)
+        sr01 = const.tile([P, 64], F32)
         sx = const.tile([P, 8], F32)
+        sx01 = const.tile([P, 8], F32)
         x_sb = const.tile([P, NB, 4, NW], BF16)
         x_t = const.tile([P, 8, NC], BF16)
 
-        w_raw = []
-        d_raw = []
-        for k in range(NK):
-            wr = raw.tile([P, 4, NJ], BF16, name="w_raw%d" % k, tag="w_raw")
-            nc.sync.dma_start(out=wr[:], in_=W_dec[k].rearrange("(p t) j -> p t j", t=4))
-            w_raw.append(wr)
-            dr = raw.tile([P, NB, 4, NW], BF16, name="d_raw%d" % k, tag="d_raw")
-            dst = dr[:].rearrange("q b (u e) w -> q (b u) (e w)", u=2)
-            if k == 0:
-                for bp in range(2):
-                    nc.sync.dma_start(
-                        out=dst[:, 4 * bp : 4 * bp + 4, :],
-                        in_=d[k, 2 * bp : 2 * bp + 2].rearrange("b (u q e) h w -> q (b u) (e h w)", u=2, q=P, e=2),
-                    )
-                nc.sync.dma_start(
-                    out=x_sb[:].rearrange("p b t w -> p b (t w)"),
-                    in_=x.rearrange("b (p t) h w -> p b (t h w)", t=4),
-                )
-            else:
-                nc.sync.dma_start(out=dst, in_=d[k].rearrange("b (u q e) h w -> q (b u) (e h w)", u=2, q=P, e=2))
-            d_raw.append(dr)
-
         state = {}
 
-        def w_transposes(k):
-            wf = w_raw[k][:].bitcast(F32)
-            banks = []
+        def load_w(k):
+            wr = raw.tile([P, 4, NJ], BF16, name="w_raw%d" % k, tag="w_raw")
+            nc.sync.dma_start(out=wr[:], in_=W_dec[k].rearrange("(p t) j -> p t j", t=4))
+            state[("w_raw", k)] = wr
+
+        def load_d(k, bp):
+            if bp == 0:
+                dr_new = raw.tile([P, NB, 4, NW], BF16, name="d_raw%d" % k, tag="d_raw")
+                state[("d_raw", k)] = dr_new
+            dr = state[("d_raw", k)]
+            nc.sync.dma_start(
+                out=dr[:, 2 * bp : 2 * bp + 2].rearrange("q b (u e) w -> q (b u) (e w)", u=2),
+                in_=d[k, 2 * bp : 2 * bp + 2].rearrange("b (u q e) h w -> q (b u) (e h w)", u=2, q=P, e=2),
+            )
+
+        def load_x(bp):
+            nc.sync.dma_start(
+                out=x_sb[:, 2 * bp : 2 * bp + 2].rearrange("p b t w -> p b (t w)"),
+                in_=x[2 * bp : 2 * bp + 2].rearrange("b (p t) h w -> p b (t h w)", t=4),
+            )
+
+        load_w(0)
+        load_d(0, 0)
+        load_x(0)
+        load_d(0, 1)
+        load_x(1)
+        for k in range(1, NK):
+            load_w(k)
+            load_d(k, 0)
+            load_d(k, 1)
+
+        def w_t(k):
+            wf = state[("w_raw", k)][:].bitcast(F32)
             for g in range(2):
                 wt = aux.tile([P, 4, P], F32, name="wt%d_%d" % (k, g), tag="aux")
                 for tt in range(2):
                     for u in range(2):
                         nc.tensor.transpose(wt[:, tt * 2 + u, :], wf[:, 2 * g + tt, u * P : (u + 1) * P], ident_f[:])
-                banks.append(wt)
-            wg = grp.tile([P, NC, 4], BF16, name="wg%d" % k, tag="wg", align_bytes=64)
-            wgf = wg[:].bitcast(F32)
-            for g in range(2):
-                nc.scalar.copy(
-                    out=wgf[:, g * 256 : (g + 1) * 256, :].rearrange("q (tt p) u -> q tt p u", tt=2),
-                    in_=banks[g][:].rearrange("q (tt u) p -> q tt p u", u=2),
-                )
-            state[("wg", k)] = wg
+                state[("wt", k, g)] = wt
+
+        def w_exit(k, g):
+            if g == 0:
+                wg_new = grp.tile([P, NC, 4], BF16, name="wg%d" % k, tag="wg", align_bytes=64)
+                state[("wg", k)] = wg_new
+            wgf = state[("wg", k)][:].bitcast(F32)
+            nc.scalar.copy(
+                out=wgf[:, g * 256 : (g + 1) * 256, :].rearrange("q (tt p) u -> q tt p u", tt=2),
+                in_=state[("wt", k, g)][:].rearrange("q (tt u) p -> q tt p u", u=2),
+            )
 
         def q_w(k):
             wg = state[("wg", k)]
@@ -109,24 +116,23 @@ def tile_cssrclassifier_pa_kernel(tc, d, W_dec, x, out_0, out_1, out_2):
 
         def d_views(k):
             if ("dg", k) not in state:
-                dg = grp.tile([P, NB, NW, 4], BF16, name="dg%d" % k, tag="dg", align_bytes=64)
-                state[("dg", k)] = dg
-            dg = state[("dg", k)]
-            src = d_raw[k][:].rearrange("q b t (c i) -> q b c t i", i=4)
-            dst = dg[:].rearrange("q b (c i) t -> q b c t i", i=4)
+                dg_new = grp.tile([P, NB, NW, 4], BF16, name="dg%d" % k, tag="dg", align_bytes=64)
+                state[("dg", k)] = dg_new
+            src = state[("d_raw", k)][:].rearrange("q b t (c i) -> q b c t i", i=4)
+            dst = state[("dg", k)][:].rearrange("q b (c i) t -> q b c t i", i=4)
             return src, dst
 
-        def rg_v01(k):
+        def rg_v(k, b0, b1):
             src, dst = d_views(k)
-            nc.vector.tensor_copy(out=dst[:, 0:2], in_=src[:, 0:2])
+            if b1 - b0 == 1:
+                nc.vector.tensor_copy(out=dst[:, b0], in_=src[:, b0])
+            else:
+                nc.vector.tensor_copy(out=dst[:, b0:b1], in_=src[:, b0:b1])
 
-        def rg_v2(k):
+        def rg_s(k, b, half):
             src, dst = d_views(k)
-            nc.vector.tensor_copy(out=dst[:, 2], in_=src[:, 2])
-
-        def rg_s3(k):
-            src, dst = d_views(k)
-            nc.scalar.copy(out=dst[:, 3], in_=src[:, 3])
+            cs = slice(half * 32, (half + 1) * 32)
+            nc.scalar.copy(out=dst[:, b, cs], in_=src[:, b, cs])
 
         def q_d(k, bp):
             if ("dc", k) not in state:
@@ -134,31 +140,32 @@ def tile_cssrclassifier_pa_kernel(tc, d, W_dec, x, out_0, out_1, out_2):
                 ds_new = mx.tile([P, NB * NW], U8, name="ds%d" % k, tag="ds", align_bytes=64)
                 state[("dc", k)] = dc_new
                 state[("ds", k)] = ds_new
-            dc = state[("dc", k)]
-            ds = state[("ds", k)]
-            dg = state[("dg", k)]
             cols = slice(bp * 512, (bp + 1) * 512)
             nc.vector.quantize_mx(
-                out=dc[:, cols].bitcast(FP8X4),
-                scales=ds[:, cols],
-                in_=dg[:, 2 * bp : 2 * bp + 2].rearrange("q b w t -> q (b w t)"),
+                out=state[("dc", k)][:, cols].bitcast(FP8X4),
+                scales=state[("ds", k)][:, cols],
+                in_=state[("dg", k)][:, 2 * bp : 2 * bp + 2].rearrange("q b w t -> q (b w t)"),
             )
 
-        def x_path():
-            for i in range(8):
-                b, h = divmod(i, 2)
-                xp = aux.tile([P, NC], BF16, name="xp%d" % i, tag="aux")
+        def x_tr(b):
+            xp = aux.tile([P, 2, NC], BF16, name="xp%d" % b, tag="aux")
+            for h in range(2):
                 for t in range(4):
-                    nc.tensor.transpose(xp[:, t * P : (t + 1) * P], x_sb[:, b, t, h * P : (h + 1) * P], ident_b[:])
-                nc.scalar.activation(out=x_t[:, i, :], in_=xp[:], func=ACT.Copy, accum_out=sx[:, i : i + 1])
+                    nc.tensor.transpose(xp[:, h, t * P : (t + 1) * P], x_sb[:, b, t, h * P : (h + 1) * P], ident_b[:])
+            state[("xp", b)] = xp
 
-        def path_a(k, i):
+        def x_exit(b):
+            xp = state[("xp", b)]
+            for h in range(2):
+                i = 2 * b + h
+                nc.scalar.activation(out=x_t[:, i, :], in_=xp[:, h, :], func=ACT.Copy, accum_out=sx[:, i : i + 1])
+
+        def ops(k):
+            return state[("wc", k)], state[("ws", k)], state[("dc", k)], state[("ds", k)]
+
+        def mm_a(k, i):
             bp, t = divmod(i, 4)
-            wc, ws, dc, ds = state[("wc", k)], state[("ws", k)], state[("dc", k)], state[("ds", k)]
-            if t == 0:
-                rec_new = recp.tile([P, 2, 4, NW], F32, name="rec%d_%d" % (k, bp), tag="rec")
-                state["rec"] = rec_new
-            rec = state["rec"]
+            wc, ws, dc, ds = ops(k)
             pa = ps_a.tile([P, 512], F32, name="pa%d_%d" % (k, i), tag="pa")
             mc = slice(t * P, (t + 1) * P)
             ncol = slice(bp * 512, (bp + 1) * 512)
@@ -171,18 +178,24 @@ def tile_cssrclassifier_pa_kernel(tc, d, W_dec, x, out_0, out_1, out_2):
                 start=True,
                 stop=True,
             )
-            nc.scalar.copy(out=rec[:, :, t, :], in_=pa[:].rearrange("p (b w) -> p b w", b=2))
+            state[("pa", k, i)] = pa
+
+        def copy_a(k, i, eng):
+            bp, t = divmod(i, 4)
+            if t == 0:
+                rec_new = recp.tile([P, 2, 4, NW], F32, name="rec%d_%d" % (k, bp), tag="rec")
+                state["rec"] = rec_new
+            rec = state["rec"]
+            nc.scalar.copy(out=rec[:, :, t, :], in_=state[("pa", k, i)][:].rearrange("p (b w) -> p b w", b=2))
             if t == 3:
-                store_eng.dma_start(
+                eng.dma_start(
                     out=out_2[2 * bp : 2 * bp + 2, k].rearrange("b (p t) h w -> p b (t h w)", t=4),
                     in_=rec[:].rearrange("p b t w -> p b (t w)"),
                 )
 
-        def path_b(k, i):
-            b, h = divmod(i, 2)
-            wc, ws, dc, ds = state[("wc", k)], state[("ws", k)], state[("dc", k)], state[("ds", k)]
+        def mm_b(k, i):
+            wc, ws, dc, ds = ops(k)
             mc = slice(i * P, (i + 1) * P)
-            col = b * 16 + k * 2 + h
             pb = ps_b.tile([P, 512], F32, name="pb%d_%d" % (k, i), tag="pb")
             nc.tensor.matmul_mx(
                 out=pb[:],
@@ -193,70 +206,120 @@ def tile_cssrclassifier_pa_kernel(tc, d, W_dec, x, out_0, out_1, out_2):
                 start=True,
                 stop=True,
             )
+            state[("pb", k, i)] = pb
             g = i % 4
             if g == 0:
                 pc_new = aux.tile([P, 4, P], F32, name="pc%d_%d" % (k, i), tag="aux")
-                state["pc"] = pc_new
-            pc = state["pc"]
+                state[("pc", k, i // 4)] = pc_new
+            pc = state[("pc", k, i // 4)]
             for t in range(4):
-                tc_ = slice(t * P, (t + 1) * P)
+                tcol = slice(t * P, (t + 1) * P)
                 nc.tensor.matmul_mx(
                     out=pc[:, g, :],
                     lhsT=dc[:, mc].bitcast(FP8X4),
                     lhsT_scale=ds[:, mc],
-                    rhs=wc[:, tc_].bitcast(FP8X4),
-                    rhs_scale=ws[:, tc_],
+                    rhs=wc[:, tcol].bitcast(FP8X4),
+                    rhs_scale=ws[:, tcol],
                     start=(t == 0),
                     stop=(t == 3),
                 )
+
+        def col_of(k, i):
+            return (i // 2) * 16 + k * 2 + (i % 2)
+
+        def stt(k, i):
+            col = col_of(k, i)
             jk = junk.tile([P, 512], BF16, name="jk%d_%d" % (k, i), tag="jk")
             nc.vector.scalar_tensor_tensor(
                 out=jk[:],
-                in0=pb[:],
+                in0=state[("pb", k, i)][:],
                 scalar=1.0,
                 in1=x_t[:, i, :],
                 op0=ALU.mult,
                 op1=ALU.max,
                 accum_out=smax[:, col : col + 1],
             )
-            if g == 3:
-                for gg in range(4):
-                    ii = i - 3 + gg
-                    cc = (ii // 2) * 16 + k * 2 + (ii % 2)
-                    jc = junk.tile([P, P], BF16, name="jc%d_%d" % (k, ii), tag="jc")
-                    nc.scalar.activation(out=jc[:], in_=pc[:, gg, :], func=ACT.Copy, accum_out=sr[:, cc : cc + 1])
 
-        w_transposes(0)
-        rg_v01(0)
-        rg_v2(0)
-        rg_s3(0)
+        def cacc(k, grp_i):
+            pc = state[("pc", k, grp_i)]
+            for gg in range(4):
+                col = col_of(k, grp_i * 4 + gg)
+                jc = junk.tile([P, P], BF16, name="jc%d_%d_%d" % (k, grp_i, gg), tag="jc")
+                nc.scalar.activation(
+                    out=jc[:], in_=pc[:, gg, :], func=ACT.Copy, scale=0.1, accum_out=sr01[:, col : col + 1]
+                )
+
+        w_t(0)
+        w_exit(0, 0)
+        w_exit(0, 1)
+        x_tr(0)
+        x_tr(1)
+        x_exit(0)
+        x_exit(1)
+        rg_v(0, 0, 1)
+        rg_v(0, 1, 2)
         q_w(0)
         q_d(0, 0)
-        q_d(0, 1)
 
-        total = NK * 8
-        for s in range(total + LEAD):
-            if s < total:
-                path_a(s // 8, s % 8)
-            if s == LEAD - 1:
-                x_path()
-            if s >= LEAD:
-                path_b((s - LEAD) // 8, (s - LEAD) % 8)
-            k, i = divmod(s, 8)
-            if k + 1 < NK:
-                if i == 0:
-                    rg_v01(k + 1)
-                elif i == 1:
-                    w_transposes(k + 1)
+        for k in range(NK - 1):
+            for i in range(8):
+                mm_b(k, i)
+                mm_a(k, i)
+                stt(k, i)
+                copy_a(k, i, nc.gpsimd)
+                if k == 0:
+                    if i == 0:
+                        x_tr(2)
+                        x_tr(3)
+                        x_exit(2)
+                        rg_v(0, 2, 4)
+                    elif i == 1:
+                        x_exit(3)
+                    elif i == 2:
+                        q_d(0, 1)
+                    elif i == 3:
+                        nc.vector.tensor_scalar_mul(out=sx01[:], in0=sx[:], scalar1=0.1)
+                else:
+                    if i == 0:
+                        cacc(k - 1, 1)
+                    elif i == 1:
+                        q_d(k, 1)
+                if i == 1:
+                    w_t(k + 1)
                 elif i == 2:
-                    rg_v2(k + 1)
-                    rg_s3(k + 1)
+                    w_exit(k + 1, 0)
+                elif i == 3:
+                    w_exit(k + 1, 1)
+                    rg_v(k + 1, 0, 1)
                 elif i == 4:
-                    q_w(k + 1)
+                    cacc(k, 0)
+                    rg_v(k + 1, 1, 2)
                 elif i == 5:
+                    rg_s(k + 1, 3, 0)
+                    q_w(k + 1)
+                elif i == 6:
+                    rg_s(k + 1, 3, 1)
                     q_d(k + 1, 0)
                 elif i == 7:
-                    q_d(k + 1, 1)
+                    rg_v(k + 1, 2, 3)
+
+        k = NK - 1
+        for g in range(4):
+            mm_b(k, 2 * g)
+            mm_b(k, 2 * g + 1)
+            mm_a(k, g)
+            stt(k, 2 * g)
+            stt(k, 2 * g + 1)
+            copy_a(k, g, nc.sync)
+            if g == 0:
+                cacc(k - 1, 1)
+                q_d(k, 1)
+            elif g == 2:
+                cacc(k, 0)
+        cacc(k, 1)
+        for i in range(4, 8):
+            mm_a(k, i)
+            copy_a(k, i, nc.scalar)
 
         def v4(ap):
             return ap.rearrange("p (b k h) -> p b k h", b=NB, k=NK, h=2)
@@ -264,50 +327,43 @@ def tile_cssrclassifier_pa_kernel(tc, d, W_dec, x, out_0, out_1, out_2):
         def bc(ap):
             return ap.rearrange("p (b h) -> p b h", h=2).unsqueeze(2).to_broadcast([P, NB, NK, 2])
 
+        def by_group(ap):
+            return ap.rearrange("p (b k h) -> p b h k", b=NB, k=NK, h=2)
+
+        def groups(ap):
+            return ap.rearrange("p (b h) -> p b h", h=2)
+
+        srx = const.tile([P, 64], F32)
+        nc.vector.tensor_tensor(out=v4(srx[:]), in0=v4(sr01[:]), in1=bc(sx01[:]), op=ALU.add)
         t1 = const.tile([P, 64], F32)
-        nc.vector.scalar_tensor_tensor(out=t1[:], in0=smax[:], scalar=2.0, in1=sr[:], op0=ALU.mult, op1=ALU.subtract)
-        t2 = const.tile([P, 64], F32)
-        nc.vector.tensor_tensor(out=v4(t2[:]), in0=v4(t1[:]), in1=bc(sx[:]), op=ALU.subtract)
-        lg0 = const.tile([P, 64], F32)
-        nc.vector.tensor_scalar(out=lg0[:], in0=t2[:], scalar1=-0.1, scalar2=-500.0, op0=ALU.mult, op1=ALU.max)
+        nc.vector.scalar_tensor_tensor(out=t1[:], in0=smax[:], scalar=-0.2, in1=srx[:], op0=ALU.mult, op1=ALU.add)
         lg = const.tile([P, 64], F32)
-        nc.vector.tensor_scalar_min(out=lg[:], in0=lg0[:], scalar1=500.0)
+        nc.vector.tensor_scalar(out=lg[:], in0=t1[:], scalar1=-500.0, scalar2=500.0, op0=ALU.max, op1=ALU.min)
         mxk = const.tile([P, 8], F32)
-        nc.vector.tensor_reduce(
-            out=mxk[:].rearrange("p (b h) -> p b h", h=2),
-            in_=lg[:].rearrange("p (b k h) -> p b h k", b=NB, k=NK, h=2),
-            axis=AX.X,
-            op=ALU.max,
-        )
+        nc.vector.tensor_reduce(out=groups(mxk[:]), in_=by_group(lg[:]), axis=AX.X, op=ALU.max)
         sh = const.tile([P, 64], F32)
         nc.vector.tensor_tensor(out=v4(sh[:]), in0=v4(lg[:]), in1=bc(mxk[:]), op=ALU.subtract)
         ex = const.tile([P, 64], F32)
         nc.scalar.activation(out=ex[:], in_=sh[:], func=ACT.Exp)
         den = const.tile([P, 8], F32)
-        nc.vector.tensor_reduce(
-            out=den[:].rearrange("p (b h) -> p b h", h=2),
-            in_=ex[:].rearrange("p (b k h) -> p b h k", b=NB, k=NK, h=2),
-            axis=AX.X,
-            op=ALU.add,
-        )
+        nc.vector.tensor_reduce(out=groups(den[:]), in_=by_group(ex[:]), axis=AX.X, op=ALU.add)
         rden = const.tile([P, 8], F32)
         nc.vector.reciprocal(out=rden[:], in_=den[:])
         nc.vector.tensor_tensor(out=v4(pad[:, 0:64]), in0=v4(ex[:]), in1=bc(rden[:]), op=ALU.mult)
         pt = aux.tile([P, P], F32, name="pt", tag="aux")
         nc.tensor.transpose(pt[:], pad[:], ident_f[:])
-        p_out = const.tile([P, P], F32)
-        nc.vector.tensor_copy(out=p_out[:], in_=pt[:])
-        nc.sync.dma_start(out=out_0.rearrange("b k (h r) w -> (b k h) (r w)", h=2), in_=p_out[0:64, :])
-
         lsum = const.tile([P, 32], F32)
         lg3 = lg[:].rearrange("p (c h) -> p c h", h=2)
         nc.vector.tensor_tensor(out=lsum[:], in0=lg3[:, :, 0], in1=lg3[:, :, 1], op=ALU.add)
-        pe_ = aux.tile([P, 32], F32, name="pe_", tag="aux")
-        nc.tensor.matmul(out=pe_[:], lhsT=ones_f[:], rhs=lsum[:], start=True, stop=True)
+        pmean = aux.tile([P, 32], F32, name="pmean", tag="aux")
+        nc.tensor.matmul(out=pmean[:], lhsT=ones_f[:], rhs=lsum[:], start=True, stop=True)
+        p_out = const.tile([P, P], F32)
+        nc.vector.tensor_copy(out=p_out[:], in_=pt[:])
+        nc.sync.dma_start(out=out_0.rearrange("b k (h r) w -> (b k h) (r w)", h=2), in_=p_out[0:64, :])
         e_sel = const.tile([P, NB, NK], F32)
         nc.vector.tensor_tensor(
             out=e_sel[:],
-            in0=pe_[:].rearrange("p (b k) -> p b k", b=NB),
+            in0=pmean[:].rearrange("p (b k) -> p b k", b=NB),
             in1=ident_f[:, 0:NB].unsqueeze(2).to_broadcast([P, NB, NK]),
             op=ALU.mult,
         )

@@ -16,7 +16,7 @@ P = 128
 NK, NB, NC, NJ, NW = 8, 4, 512, 512, 256
 FLOPS = 2 * NK * NB * NC * NJ * NW
 
-MANUAL = True
+MANUAL = False
 
 
 def tile_cssrclassifier_pa_kernel(tc, d, W_dec, x, out_0, out_1, out_2):
@@ -129,10 +129,12 @@ def tile_cssrclassifier_pa_kernel(tc, d, W_dec, x, out_0, out_1, out_2):
             else:
                 nc.vector.tensor_copy(out=dst[:, b0:b1], in_=src[:, b0:b1])
 
-        def rg_s(k, b, half):
+        def rg_g(k, b, half):
             src, dst = d_views(k)
             cs = slice(half * 32, (half + 1) * 32)
-            nc.scalar.copy(out=dst[:, b, cs], in_=src[:, b, cs])
+            nc.gpsimd.tensor_scalar(
+                out=dst[:, b, cs], in0=src[:, b, cs], scalar1=1.0, scalar2=0.0, op0=ALU.mult, op1=ALU.add
+            )
 
         def q_d(k, bp):
             if ("dc", k) not in state:
@@ -288,6 +290,9 @@ def tile_cssrclassifier_pa_kernel(tc, d, W_dec, x, out_0, out_1, out_2):
                     w_t(k + 1)
                 elif i == 2:
                     w_exit(k + 1, 0)
+                    for b in (2, 3):
+                        for half in range(2):
+                            rg_g(k + 1, b, half)
                 elif i == 3:
                     w_exit(k + 1, 1)
                     rg_v(k + 1, 0, 1)
@@ -295,13 +300,9 @@ def tile_cssrclassifier_pa_kernel(tc, d, W_dec, x, out_0, out_1, out_2):
                     cacc(k, 0)
                     rg_v(k + 1, 1, 2)
                 elif i == 5:
-                    rg_s(k + 1, 3, 0)
                     q_w(k + 1)
                 elif i == 6:
-                    rg_s(k + 1, 3, 1)
                     q_d(k + 1, 0)
-                elif i == 7:
-                    rg_v(k + 1, 2, 3)
 
         k = NK - 1
         for g in range(4):

@@ -28,9 +28,9 @@ def tile_cssrclassifier_pa_kernel(tc, d, W_dec, x, out_0, out_1, out_2):
         mx = ctx.enter_context(tc.tile_pool(name="mx", bufs=3))
         recp = ctx.enter_context(tc.tile_pool(name="recp", bufs=4))
         junk = ctx.enter_context(tc.tile_pool(name="junk", bufs=2))
-        ps_a = ctx.enter_context(tc.psum_pool(name="ps_a", bufs=2))
         ps_b = ctx.enter_context(tc.psum_pool(name="ps_b", bufs=3))
-        aux = ctx.enter_context(tc.psum_pool(name="aux", bufs=3))
+        aux = ctx.enter_context(tc.psum_pool(name="aux", bufs=5))
+        ps_a = aux
         if MANUAL:
             ctx.enter_context(tc.manual_schedule())
 
@@ -129,12 +129,10 @@ def tile_cssrclassifier_pa_kernel(tc, d, W_dec, x, out_0, out_1, out_2):
             else:
                 nc.vector.tensor_copy(out=dst[:, b0:b1], in_=src[:, b0:b1])
 
-        def rg_g(k, b, half):
+        def rg_s(k, b, half):
             src, dst = d_views(k)
             cs = slice(half * 32, (half + 1) * 32)
-            nc.gpsimd.tensor_scalar(
-                out=dst[:, b, cs], in0=src[:, b, cs], scalar1=1.0, scalar2=0.0, op0=ALU.mult, op1=ALU.add
-            )
+            nc.scalar.copy(out=dst[:, b, cs], in_=src[:, b, cs])
 
         def q_d(k, bp):
             if ("dc", k) not in state:
@@ -168,7 +166,7 @@ def tile_cssrclassifier_pa_kernel(tc, d, W_dec, x, out_0, out_1, out_2):
         def mm_a(k, i):
             bp, t = divmod(i, 4)
             wc, ws, dc, ds = ops(k)
-            pa = ps_a.tile([P, 512], F32, name="pa%d_%d" % (k, i), tag="pa")
+            pa = ps_a.tile([P, 512], F32, name="pa%d_%d" % (k, i), tag="aux")
             mc = slice(t * P, (t + 1) * P)
             ncol = slice(bp * 512, (bp + 1) * 512)
             nc.tensor.matmul_mx(
@@ -290,9 +288,6 @@ def tile_cssrclassifier_pa_kernel(tc, d, W_dec, x, out_0, out_1, out_2):
                     w_t(k + 1)
                 elif i == 2:
                     w_exit(k + 1, 0)
-                    for b in (2, 3):
-                        for half in range(2):
-                            rg_g(k + 1, b, half)
                 elif i == 3:
                     w_exit(k + 1, 1)
                     rg_v(k + 1, 0, 1)
@@ -300,9 +295,13 @@ def tile_cssrclassifier_pa_kernel(tc, d, W_dec, x, out_0, out_1, out_2):
                     cacc(k, 0)
                     rg_v(k + 1, 1, 2)
                 elif i == 5:
+                    rg_s(k + 1, 3, 0)
                     q_w(k + 1)
                 elif i == 6:
+                    rg_s(k + 1, 3, 1)
                     q_d(k + 1, 0)
+                elif i == 7:
+                    rg_v(k + 1, 2, 3)
 
         k = NK - 1
         for g in range(4):

@@ -132,7 +132,9 @@ def tile_cssrclassifier_pa_kernel(tc, d, W_dec, x, out_0, out_1, out_2):
         def rg_s(k, b, half):
             src, dst = d_views(k)
             cs = slice(half * 32, (half + 1) * 32)
-            nc.scalar.copy(out=dst[:, b, cs], in_=src[:, b, cs])
+            nc.gpsimd.tensor_scalar(
+                out=dst[:, b, cs], in0=src[:, b, cs], scalar1=1.0, scalar2=0.0, op0=ALU.mult, op1=ALU.add
+            )
 
         def q_d(k, bp):
             if ("dc", k) not in state:
@@ -288,6 +290,8 @@ def tile_cssrclassifier_pa_kernel(tc, d, W_dec, x, out_0, out_1, out_2):
                     w_t(k + 1)
                 elif i == 2:
                     w_exit(k + 1, 0)
+                    rg_s(k + 1, 3, 0)
+                    rg_s(k + 1, 3, 1)
                 elif i == 3:
                     w_exit(k + 1, 1)
                     rg_v(k + 1, 0, 1)
@@ -295,10 +299,8 @@ def tile_cssrclassifier_pa_kernel(tc, d, W_dec, x, out_0, out_1, out_2):
                     cacc(k, 0)
                     rg_v(k + 1, 1, 2)
                 elif i == 5:
-                    rg_s(k + 1, 3, 0)
                     q_w(k + 1)
                 elif i == 6:
-                    rg_s(k + 1, 3, 1)
                     q_d(k + 1, 0)
                 elif i == 7:
                     rg_v(k + 1, 2, 3)

@@ -44,12 +44,13 @@ def tile_cssrclassifier_pa_kernel(tc, d, W_dec, x, out_0, out_1, out_2):
         make_identity(nc, ident_b[:])
         ones_f = const.tile([P, P], F32)
         nc.vector.memset(ones_f[:], 1.0 / NW)
+        ones_b = const.tile([P, 32], BF16)
+        nc.vector.memset(ones_b[:], 1.0)
         pad = const.tile([P, P], F32)
         nc.vector.memset(pad[:], 0.0)
 
         smax = const.tile([P, 64], F32)
         sr01 = const.tile([P, 64], F32)
-        sx = const.tile([P, 8], F32)
         sx01 = const.tile([P, 8], F32)
         x_sb = const.tile([P, NB, 4, NW], BF16)
         x_t = const.tile([P, 8, NC], BF16)
@@ -132,9 +133,7 @@ def tile_cssrclassifier_pa_kernel(tc, d, W_dec, x, out_0, out_1, out_2):
         def rg_s(k, b, half):
             src, dst = d_views(k)
             cs = slice(half * 32, (half + 1) * 32)
-            nc.gpsimd.tensor_scalar(
-                out=dst[:, b, cs], in0=src[:, b, cs], scalar1=1.0, scalar2=0.0, op0=ALU.mult, op1=ALU.add
-            )
+            nc.scalar.copy(out=dst[:, b, cs], in_=src[:, b, cs])
 
         def q_d(k, bp):
             if ("dc", k) not in state:
@@ -156,11 +155,25 @@ def tile_cssrclassifier_pa_kernel(tc, d, W_dec, x, out_0, out_1, out_2):
                     nc.tensor.transpose(xp[:, h, t * P : (t + 1) * P], x_sb[:, b, t, h * P : (h + 1) * P], ident_b[:])
             state[("xp", b)] = xp
 
+        def x_sum(bp):
+            xs = aux.tile([P, 4, 32], F32, name="xs%d" % bp, tag="aux")
+            for g in range(4):
+                b, h = 2 * bp + g // 2, g % 2
+                for t in range(4):
+                    nc.tensor.matmul(
+                        out=xs[:, g, :],
+                        lhsT=x_sb[:, b, t, h * P : (h + 1) * P],
+                        rhs=ones_b[:],
+                        start=(t == 0),
+                        stop=(t == 3),
+                    )
+            state[("xs", bp)] = xs
+
         def x_exit(b):
-            xp = state[("xp", b)]
-            for h in range(2):
-                i = 2 * b + h
-                nc.scalar.activation(out=x_t[:, i, :], in_=xp[:, h, :], func=ACT.Copy, accum_out=sx[:, i : i + 1])
+            nc.scalar.copy(out=x_t[:, 2 * b : 2 * b + 2, :], in_=state[("xp", b)][:])
+
+        def x_sum_exit(bp):
+            nc.scalar.mul(out=sx01[:, 4 * bp : 4 * bp + 4], in_=state[("xs", bp)][:, :, 0], mul=0.1)
 
         def ops(k):
             return state[("wc", k)], state[("ws", k)], state[("dc", k)], state[("ds", k)]
@@ -189,7 +202,14 @@ def tile_cssrclassifier_pa_kernel(tc, d, W_dec, x, out_0, out_1, out_2):
                 state["rec"] = rec_new
             rec = state["rec"]
             nc.scalar.copy(out=rec[:, :, t, :], in_=state[("pa", k, i)][:].rearrange("p (b w) -> p b w", b=2))
-            if t == 3:
+            if k == NK - 1 and bp == 1:
+                if t % 2 == 1:
+                    ts = slice(t - 1, t + 1)
+                    eng.dma_start(
+                        out=out_2[2 * bp : 2 * bp + 2, k].rearrange("b (p t) h w -> p b t (h w)", t=4)[:, :, ts, :],
+                        in_=rec[:, :, ts, :],
+                    )
+            elif t == 3:
                 eng.dma_start(
                     out=out_2[2 * bp : 2 * bp + 2, k].rearrange("b (p t) h w -> p b (t h w)", t=4),
                     in_=rec[:].rearrange("p b t w -> p b (t w)"),
@@ -258,6 +278,8 @@ def tile_cssrclassifier_pa_kernel(tc, d, W_dec, x, out_0, out_1, out_2):
         x_tr(1)
         x_exit(0)
         x_exit(1)
+        x_sum(0)
+        x_sum_exit(0)
         rg_v(0, 0, 1)
         rg_v(0, 1, 2)
         q_w(0)
@@ -277,33 +299,46 @@ def tile_cssrclassifier_pa_kernel(tc, d, W_dec, x, out_0, out_1, out_2):
                         rg_v(0, 2, 4)
                     elif i == 1:
                         x_exit(3)
+                        x_sum(1)
+                        w_t(1)
                     elif i == 2:
+                        x_sum_exit(1)
                         q_d(0, 1)
+                        w_exit(1, 0)
                     elif i == 3:
-                        nc.vector.tensor_scalar_mul(out=sx01[:], in0=sx[:], scalar1=0.1)
+                        w_exit(1, 1)
+                        rg_v(1, 0, 2)
+                    elif i == 4:
+                        cacc(0, 0)
+                        rg_v(1, 2, 3)
+                    elif i == 5:
+                        rg_s(1, 3, 0)
+                        q_w(1)
+                    elif i == 6:
+                        rg_s(1, 3, 1)
+                        q_d(1, 0)
                 else:
                     if i == 0:
+                        w_t(k + 1)
                         cacc(k - 1, 1)
+                        rg_v(k + 1, 0, 2)
                     elif i == 1:
-                        q_d(k, 1)
-                if i == 1:
-                    w_t(k + 1)
-                elif i == 2:
-                    w_exit(k + 1, 0)
-                    rg_s(k + 1, 3, 0)
-                    rg_s(k + 1, 3, 1)
-                elif i == 3:
-                    w_exit(k + 1, 1)
-                    rg_v(k + 1, 0, 1)
-                elif i == 4:
-                    cacc(k, 0)
-                    rg_v(k + 1, 1, 2)
-                elif i == 5:
-                    q_w(k + 1)
-                elif i == 6:
-                    q_d(k + 1, 0)
-                elif i == 7:
-                    rg_v(k + 1, 2, 3)
+                        w_exit(k + 1, 0)
+                        if k == 1:
+                            q_d(1, 1)
+                    elif i == 2:
+                        w_exit(k + 1, 1)
+                        rg_v(k + 1, 2, 3)
+                    elif i == 3:
+                        rg_s(k + 1, 3, 0)
+                        q_w(k + 1)
+                    elif i == 4:
+                        cacc(k, 0)
+                        q_d(k + 1, 0)
+                    elif i == 5:
+                        rg_s(k + 1, 3, 1)
+                    elif i == 6:
+                        q_d(k + 1, 1)
 
         k = NK - 1
         for g in range(4):
@@ -315,7 +350,6 @@ def tile_cssrclassifier_pa_kernel(tc, d, W_dec, x, out_0, out_1, out_2):
             copy_a(k, g, nc.sync)
             if g == 0:
                 cacc(k - 1, 1)
-                q_d(k, 1)
             elif g == 2:
                 cacc(k, 0)
         cacc(k, 1)

@@ -24,13 +24,13 @@ def tile_cssrclassifier_pa_kernel(tc, d, W_dec, x, out_0, out_1, out_2):
     with ExitStack() as ctx:
         const = ctx.enter_context(tc.tile_pool(name="const", bufs=1))
         raw = ctx.enter_context(tc.tile_pool(name="raw", bufs=NK))
-        grp = ctx.enter_context(tc.tile_pool(name="grp", bufs=2))
+        grp = ctx.enter_context(tc.tile_pool(name="grp", bufs=3))
         mx = ctx.enter_context(tc.tile_pool(name="mx", bufs=3))
-        recp = ctx.enter_context(tc.tile_pool(name="recp", bufs=4))
+        recp = ctx.enter_context(tc.tile_pool(name="recp", bufs=6))
         junk = ctx.enter_context(tc.tile_pool(name="junk", bufs=2))
-        ps_b = ctx.enter_context(tc.psum_pool(name="ps_b", bufs=3))
-        aux = ctx.enter_context(tc.psum_pool(name="aux", bufs=5))
+        aux = ctx.enter_context(tc.psum_pool(name="aux", bufs=8))
         ps_a = aux
+        ps_b = aux
         if MANUAL:
             ctx.enter_context(tc.manual_schedule())
 
@@ -44,13 +44,12 @@ def tile_cssrclassifier_pa_kernel(tc, d, W_dec, x, out_0, out_1, out_2):
         make_identity(nc, ident_b[:])
         ones_f = const.tile([P, P], F32)
         nc.vector.memset(ones_f[:], 1.0 / NW)
-        ones_b = const.tile([P, 32], BF16)
-        nc.vector.memset(ones_b[:], 1.0)
         pad = const.tile([P, P], F32)
         nc.vector.memset(pad[:], 0.0)
 
         smax = const.tile([P, 64], F32)
         sr01 = const.tile([P, 64], F32)
+        sx = const.tile([P, 8], F32)
         sx01 = const.tile([P, 8], F32)
         x_sb = const.tile([P, NB, 4, NW], BF16)
         x_t = const.tile([P, 8, NC], BF16)
@@ -155,25 +154,11 @@ def tile_cssrclassifier_pa_kernel(tc, d, W_dec, x, out_0, out_1, out_2):
                     nc.tensor.transpose(xp[:, h, t * P : (t + 1) * P], x_sb[:, b, t, h * P : (h + 1) * P], ident_b[:])
             state[("xp", b)] = xp
 
-        def x_sum(bp):
-            xs = aux.tile([P, 4, 32], F32, name="xs%d" % bp, tag="aux")
-            for g in range(4):
-                b, h = 2 * bp + g // 2, g % 2
-                for t in range(4):
-                    nc.tensor.matmul(
-                        out=xs[:, g, :],
-                        lhsT=x_sb[:, b, t, h * P : (h + 1) * P],
-                        rhs=ones_b[:],
-                        start=(t == 0),
-                        stop=(t == 3),
-                    )
-            state[("xs", bp)] = xs
-
         def x_exit(b):
-            nc.scalar.copy(out=x_t[:, 2 * b : 2 * b + 2, :], in_=state[("xp", b)][:])
-
-        def x_sum_exit(bp):
-            nc.scalar.mul(out=sx01[:, 4 * bp : 4 * bp + 4], in_=state[("xs", bp)][:, :, 0], mul=0.1)
+            xp = state[("xp", b)]
+            for h in range(2):
+                i = 2 * b + h
+                nc.scalar.activation(out=x_t[:, i, :], in_=xp[:, h, :], func=ACT.Copy, accum_out=sx[:, i : i + 1])
 
         def ops(k):
             return state[("wc", k)], state[("ws", k)], state[("dc", k)], state[("ds", k)]
@@ -202,14 +187,7 @@ def tile_cssrclassifier_pa_kernel(tc, d, W_dec, x, out_0, out_1, out_2):
                 state["rec"] = rec_new
             rec = state["rec"]
             nc.scalar.copy(out=rec[:, :, t, :], in_=state[("pa", k, i)][:].rearrange("p (b w) -> p b w", b=2))
-            if k == NK - 1 and bp == 1:
-                if t % 2 == 1:
-                    ts = slice(t - 1, t + 1)
-                    eng.dma_start(
-                        out=out_2[2 * bp : 2 * bp + 2, k].rearrange("b (p t) h w -> p b t (h w)", t=4)[:, :, ts, :],
-                        in_=rec[:, :, ts, :],
-                    )
-            elif t == 3:
+            if t == 3:
                 eng.dma_start(
                     out=out_2[2 * bp : 2 * bp + 2, k].rearrange("b (p t) h w -> p b (t h w)", t=4),
                     in_=rec[:].rearrange("p b t w -> p b (t w)"),
@@ -218,7 +196,7 @@ def tile_cssrclassifier_pa_kernel(tc, d, W_dec, x, out_0, out_1, out_2):
         def mm_b(k, i):
             wc, ws, dc, ds = ops(k)
             mc = slice(i * P, (i + 1) * P)
-            pb = ps_b.tile([P, 512], F32, name="pb%d_%d" % (k, i), tag="pb")
+            pb = ps_b.tile([P, 512], F32, name="pb%d_%d" % (k, i), tag="aux")
             nc.tensor.matmul_mx(
                 out=pb[:],
                 lhsT=dc[:, mc].bitcast(FP8X4),
@@ -278,8 +256,6 @@ def tile_cssrclassifier_pa_kernel(tc, d, W_dec, x, out_0, out_1, out_2):
         x_tr(1)
         x_exit(0)
         x_exit(1)
-        x_sum(0)
-        x_sum_exit(0)
         rg_v(0, 0, 1)
         rg_v(0, 1, 2)
         q_w(0)
@@ -299,46 +275,33 @@ def tile_cssrclassifier_pa_kernel(tc, d, W_dec, x, out_0, out_1, out_2):
                         rg_v(0, 2, 4)
                     elif i == 1:
                         x_exit(3)
-                        x_sum(1)
-                        w_t(1)
                     elif i == 2:
-                        x_sum_exit(1)
                         q_d(0, 1)
-                        w_exit(1, 0)
                     elif i == 3:
-                        w_exit(1, 1)
-                        rg_v(1, 0, 2)
-                    elif i == 4:
-                        cacc(0, 0)
-                        rg_v(1, 2, 3)
-                    elif i == 5:
-                        rg_s(1, 3, 0)
-                        q_w(1)
-                    elif i == 6:
-                        rg_s(1, 3, 1)
-                        q_d(1, 0)
+                        nc.vector.tensor_scalar_mul(out=sx01[:], in0=sx[:], scalar1=0.1)
                 else:
                     if i == 0:
-                        w_t(k + 1)
                         cacc(k - 1, 1)
-                        rg_v(k + 1, 0, 2)
                     elif i == 1:
-                        w_exit(k + 1, 0)
-                        if k == 1:
-                            q_d(1, 1)
-                    elif i == 2:
-                        w_exit(k + 1, 1)
-                        rg_v(k + 1, 2, 3)
-                    elif i == 3:
-                        rg_s(k + 1, 3, 0)
-                        q_w(k + 1)
-                    elif i == 4:
-                        cacc(k, 0)
-                        q_d(k + 1, 0)
-                    elif i == 5:
-                        rg_s(k + 1, 3, 1)
-                    elif i == 6:
-                        q_d(k + 1, 1)
+                        q_d(k, 1)
+                if i == 1:
+                    w_t(k + 1)
+                elif i == 2:
+                    w_exit(k + 1, 0)
+                elif i == 3:
+                    w_exit(k + 1, 1)
+                    rg_v(k + 1, 0, 1)
+                elif i == 4:
+                    cacc(k, 0)
+                    rg_v(k + 1, 1, 2)
+                elif i == 5:
+                    rg_s(k + 1, 3, 0)
+                    q_w(k + 1)
+                elif i == 6:
+                    rg_s(k + 1, 3, 1)
+                    q_d(k + 1, 0)
+                elif i == 7:
+                    rg_v(k + 1, 2, 3)
 
         k = NK - 1
         for g in range(4):
@@ -350,6 +313,7 @@ def tile_cssrclassifier_pa_kernel(tc, d, W_dec, x, out_0, out_1, out_2):
             copy_a(k, g, nc.sync)
             if g == 0:
                 cacc(k - 1, 1)
+                q_d(k, 1)
             elif g == 2:
                 cacc(k, 0)
         cacc(k, 1)

@@ -129,6 +129,11 @@ def tile_cssrclassifier_pa_kernel(tc, d, W_dec, x, out_0, out_1, out_2):
             else:
                 nc.vector.tensor_copy(out=dst[:, b0:b1], in_=src[:, b0:b1])
 
+        def rg_v_half(k, b, half):
+            src, dst = d_views(k)
+            cs = slice(half * 32, (half + 1) * 32)
+            nc.vector.tensor_copy(out=dst[:, b, cs], in_=src[:, b, cs])
+
         def rg_s(k, b, half):
             src, dst = d_views(k)
             cs = slice(half * 32, (half + 1) * 32)
@@ -301,7 +306,8 @@ def tile_cssrclassifier_pa_kernel(tc, d, W_dec, x, out_0, out_1, out_2):
                     rg_s(k + 1, 3, 1)
                     q_d(k + 1, 0)
                 elif i == 7:
-                    rg_v(k + 1, 2, 3)
+                    rg_s(k + 1, 2, 1)
+                    rg_v_half(k + 1, 2, 0)
 
         k = NK - 1
         for g in range(4):

from contextlib import ExitStack

import concourse.mybir as mybir
from concourse.masks import make_identity

FP8X4 = mybir.dt.float8_e4m3fn_x4
BF16 = mybir.dt.bfloat16
F32 = mybir.dt.float32
U32 = mybir.dt.uint32
U8 = mybir.dt.uint8
ALU = mybir.AluOpType
ACT = mybir.ActivationFunctionType
AX = mybir.AxisListType

P = 128
NK, NB, NC, NJ, NW = 8, 4, 512, 512, 256
FLOPS = 2 * NK * NB * NC * NJ * NW

MANUAL = False


def tile_cssrclassifier_pa_kernel(tc, d, W_dec, x, out_0, out_1, out_2):
    nc = tc.nc
    with ExitStack() as ctx:
        const = ctx.enter_context(tc.tile_pool(name="const", bufs=1))
        raw = ctx.enter_context(tc.tile_pool(name="raw", bufs=NK))
        grp = ctx.enter_context(tc.tile_pool(name="grp", bufs=3))
        mx = ctx.enter_context(tc.tile_pool(name="mx", bufs=3))
        recp = ctx.enter_context(tc.tile_pool(name="recp", bufs=6))
        junk = ctx.enter_context(tc.tile_pool(name="junk", bufs=2))
        aux = ctx.enter_context(tc.psum_pool(name="aux", bufs=8))
        ps_a = aux
        ps_b = aux
        if MANUAL:
            ctx.enter_context(tc.manual_schedule())

        warm = const.tile([P, 1], F32)
        nc.vector.memset(warm[:], 0.0)
        warm2 = const.tile([P, 1], F32)
        nc.scalar.activation(out=warm2[:], in_=warm[:], func=ACT.Exp)
        ident_f = const.tile([P, P], F32)
        make_identity(nc, ident_f[:])
        ident_b = const.tile([P, P], BF16)
        make_identity(nc, ident_b[:])
        ones_f = const.tile([P, P], F32)
        nc.vector.memset(ones_f[:], 1.0 / NW)
        pad = const.tile([P, P], F32)
        nc.vector.memset(pad[:], 0.0)

        smax = const.tile([P, 64], F32)
        sr01 = const.tile([P, 64], F32)
        sx = const.tile([P, 8], F32)
        sx01 = const.tile([P, 8], F32)
        x_sb = const.tile([P, NB, 4, NW], BF16)
        x_t = const.tile([P, 8, NC], BF16)

        state = {}

        def load_w(k):
            wr = raw.tile([P, 4, NJ], BF16, name="w_raw%d" % k, tag="w_raw")
            nc.sync.dma_start(out=wr[:], in_=W_dec[k].rearrange("(p t) j -> p t j", t=4))
            state[("w_raw", k)] = wr

        def load_d(k, bp):
            if bp == 0:
                dr_new = raw.tile([P, NB, 4, NW], BF16, name="d_raw%d" % k, tag="d_raw")
                state[("d_raw", k)] = dr_new
            dr = state[("d_raw", k)]
            nc.sync.dma_start(
                out=dr[:, 2 * bp : 2 * bp + 2].rearrange("q b (u e) w -> q (b u) (e w)", u=2),
                in_=d[k, 2 * bp : 2 * bp + 2].rearrange("b (u q e) h w -> q (b u) (e h w)", u=2, q=P, e=2),
            )

        def load_x(bp):
            nc.sync.dma_start(
                out=x_sb[:, 2 * bp : 2 * bp + 2].rearrange("p b t w -> p b (t w)"),
                in_=x[2 * bp : 2 * bp + 2].rearrange("b (p t) h w -> p b (t h w)", t=4),
            )

        load_w(0)
        load_d(0, 0)
        load_x(0)
        load_d(0, 1)
        load_x(1)
        for k in range(1, NK):
            load_w(k)
            load_d(k, 0)
            load_d(k, 1)

        def w_t(k):
            wf = state[("w_raw", k)][:].bitcast(F32)
            for g in range(2):
                wt = aux.tile([P, 4, P], F32, name="wt%d_%d" % (k, g), tag="aux")
                for tt in range(2):
                    for u in range(2):
                        nc.tensor.transpose(wt[:, tt * 2 + u, :], wf[:, 2 * g + tt, u * P : (u + 1) * P], ident_f[:])
                state[("wt", k, g)] = wt

        def w_exit(k, g):
            if g == 0:
                wg_new = grp.tile([P, NC, 4], BF16, name="wg%d" % k, tag="wg", align_bytes=64)
                state[("wg", k)] = wg_new
            wgf = state[("wg", k)][:].bitcast(F32)
            nc.scalar.copy(
                out=wgf[:, g * 256 : (g + 1) * 256, :].rearrange("q (tt p) u -> q tt p u", tt=2),
                in_=state[("wt", k, g)][:].rearrange("q (tt u) p -> q tt p u", u=2),
            )

        def q_w(k):
            wg = state[("wg", k)]
            wc = mx.tile([P, NC], U32, name="wc%d" % k, tag="wc", align_bytes=64)
            ws = mx.tile([P, NC], U8, name="ws%d" % k, tag="ws", align_bytes=64)
            nc.vector.quantize_mx(out=wc[:].bitcast(FP8X4), scales=ws[:], in_=wg[:].rearrange("q c t -> q (c t)"))
            state[("wc", k)] = wc
            state[("ws", k)] = ws

        def d_views(k):
            if ("dg", k) not in state:
                dg_new = grp.tile([P, NB, NW, 4], BF16, name="dg%d" % k, tag="dg", align_bytes=64)
                state[("dg", k)] = dg_new
            src = state[("d_raw", k)][:].rearrange("q b t (c i) -> q b c t i", i=4)
            dst = state[("dg", k)][:].rearrange("q b (c i) t -> q b c t i", i=4)
            return src, dst

        def rg_v(k, b0, b1):
            src, dst = d_views(k)
            if b1 - b0 == 1:
                nc.vector.tensor_copy(out=dst[:, b0], in_=src[:, b0])
            else:
                nc.vector.tensor_copy(out=dst[:, b0:b1], in_=src[:, b0:b1])

        def rg_v_half(k, b, half):
            src, dst = d_views(k)
            cs = slice(half * 32, (half + 1) * 32)
            nc.vector.tensor_copy(out=dst[:, b, cs], in_=src[:, b, cs])

        def rg_s(k, b, half):
            src, dst = d_views(k)
            cs = slice(half * 32, (half + 1) * 32)
            nc.scalar.copy(out=dst[:, b, cs], in_=src[:, b, cs])

        def q_d(k, bp):
            if ("dc", k) not in state:
                dc_new = mx.tile([P, NB * NW], U32, name="dc%d" % k, tag="dc", align_bytes=64)
                ds_new = mx.tile([P, NB * NW], U8, name="ds%d" % k, tag="ds", align_bytes=64)
                state[("dc", k)] = dc_new
                state[("ds", k)] = ds_new
            cols = slice(bp * 512, (bp + 1) * 512)
            nc.vector.quantize_mx(
                out=state[("dc", k)][:, cols].bitcast(FP8X4),
                scales=state[("ds", k)][:, cols],
                in_=state[("dg", k)][:, 2 * bp : 2 * bp + 2].rearrange("q b w t -> q (b w t)"),
            )

        def x_tr(b):
            xp = aux.tile([P, 2, NC], BF16, name="xp%d" % b, tag="aux")
            for h in range(2):
                for t in range(4):
                    nc.tensor.transpose(xp[:, h, t * P : (t + 1) * P], x_sb[:, b, t, h * P : (h + 1) * P], ident_b[:])
            state[("xp", b)] = xp

        def x_exit(b):
            xp = state[("xp", b)]
            for h in range(2):
                i = 2 * b + h
                nc.scalar.activation(out=x_t[:, i, :], in_=xp[:, h, :], func=ACT.Copy, accum_out=sx[:, i : i + 1])

        def ops(k):
            return state[("wc", k)], state[("ws", k)], state[("dc", k)], state[("ds", k)]

        def mm_a(k, i):
            bp, t = divmod(i, 4)
            wc, ws, dc, ds = ops(k)
            pa = ps_a.tile([P, 512], F32, name="pa%d_%d" % (k, i), tag="aux")
            mc = slice(t * P, (t + 1) * P)
            ncol = slice(bp * 512, (bp + 1) * 512)
            nc.tensor.matmul_mx(
                out=pa[:],
                lhsT=wc[:, mc].bitcast(FP8X4),
                lhsT_scale=ws[:, mc],
                rhs=dc[:, ncol].bitcast(FP8X4),
                rhs_scale=ds[:, ncol],
                start=True,
                stop=True,
            )
            state[("pa", k, i)] = pa

        def copy_a(k, i, eng):
            bp, t = divmod(i, 4)
            if t == 0:
                rec_new = recp.tile([P, 2, 4, NW], F32, name="rec%d_%d" % (k, bp), tag="rec")
                state["rec"] = rec_new
            rec = state["rec"]
            nc.scalar.copy(out=rec[:, :, t, :], in_=state[("pa", k, i)][:].rearrange("p (b w) -> p b w", b=2))
            if t == 3:
                eng.dma_start(
                    out=out_2[2 * bp : 2 * bp + 2, k].rearrange("b (p t) h w -> p b (t h w)", t=4),
                    in_=rec[:].rearrange("p b t w -> p b (t w)"),
                )

        def mm_b(k, i):
            wc, ws, dc, ds = ops(k)
            mc = slice(i * P, (i + 1) * P)
            pb = ps_b.tile([P, 512], F32, name="pb%d_%d" % (k, i), tag="aux")
            nc.tensor.matmul_mx(
                out=pb[:],
                lhsT=dc[:, mc].bitcast(FP8X4),
                lhsT_scale=ds[:, mc],
                rhs=wc[:].bitcast(FP8X4),
                rhs_scale=ws[:],
                start=True,
                stop=True,
            )
            state[("pb", k, i)] = pb
            g = i % 4
            if g == 0:
                pc_new = aux.tile([P, 4, P], F32, name="pc%d_%d" % (k, i), tag="aux")
                state[("pc", k, i // 4)] = pc_new
            pc = state[("pc", k, i // 4)]
            for t in range(4):
                tcol = slice(t * P, (t + 1) * P)
                nc.tensor.matmul_mx(
                    out=pc[:, g, :],
                    lhsT=dc[:, mc].bitcast(FP8X4),
                    lhsT_scale=ds[:, mc],
                    rhs=wc[:, tcol].bitcast(FP8X4),
                    rhs_scale=ws[:, tcol],
                    start=(t == 0),
                    stop=(t == 3),
                )

        def col_of(k, i):
            return (i // 2) * 16 + k * 2 + (i % 2)

        def stt(k, i):
            col = col_of(k, i)
            jk = junk.tile([P, 512], BF16, name="jk%d_%d" % (k, i), tag="jk")
            nc.vector.scalar_tensor_tensor(
                out=jk[:],
                in0=state[("pb", k, i)][:],
                scalar=1.0,
                in1=x_t[:, i, :],
                op0=ALU.mult,
                op1=ALU.max,
                accum_out=smax[:, col : col + 1],
            )

        def cacc(k, grp_i):
            pc = state[("pc", k, grp_i)]
            for gg in range(4):
                col = col_of(k, grp_i * 4 + gg)
                jc = junk.tile([P, P], BF16, name="jc%d_%d_%d" % (k, grp_i, gg), tag="jc")
                nc.scalar.activation(
                    out=jc[:], in_=pc[:, gg, :], func=ACT.Copy, scale=0.1, accum_out=sr01[:, col : col + 1]
                )

        w_t(0)
        w_exit(0, 0)
        w_exit(0, 1)
        x_tr(0)
        x_tr(1)
        x_exit(0)
        x_exit(1)
        rg_v(0, 0, 1)
        rg_v(0, 1, 2)
        q_w(0)
        q_d(0, 0)

        for k in range(NK - 1):
            for i in range(8):
                mm_b(k, i)
                mm_a(k, i)
                stt(k, i)
                copy_a(k, i, nc.gpsimd)
                if k == 0:
                    if i == 0:
                        x_tr(2)
                        x_tr(3)
                        x_exit(2)
                        rg_v(0, 2, 4)
                    elif i == 1:
                        x_exit(3)
                    elif i == 2:
                        q_d(0, 1)
                    elif i == 3:
                        nc.vector.tensor_scalar_mul(out=sx01[:], in0=sx[:], scalar1=0.1)
                else:
                    if i == 0:
                        cacc(k - 1, 1)
                    elif i == 1:
                        q_d(k, 1)
                if i == 1:
                    w_t(k + 1)
                elif i == 2:
                    w_exit(k + 1, 0)
                elif i == 3:
                    w_exit(k + 1, 1)
                    rg_v(k + 1, 0, 1)
                elif i == 4:
                    cacc(k, 0)
                    rg_v(k + 1, 1, 2)
                elif i == 5:
                    rg_s(k + 1, 3, 0)
                    q_w(k + 1)
                elif i == 6:
                    rg_s(k + 1, 3, 1)
                    q_d(k + 1, 0)
                elif i == 7:
                    rg_s(k + 1, 2, 1)
                    rg_v_half(k + 1, 2, 0)

        k = NK - 1
        for g in range(4):
            mm_b(k, 2 * g)
            mm_b(k, 2 * g + 1)
            mm_a(k, g)
            stt(k, 2 * g)
            stt(k, 2 * g + 1)
            copy_a(k, g, nc.sync)
            if g == 0:
                cacc(k - 1, 1)
                q_d(k, 1)
            elif g == 2:
                cacc(k, 0)
        cacc(k, 1)
        for i in range(4, 8):
            mm_a(k, i)
            copy_a(k, i, nc.scalar)

        def v4(ap):
            return ap.rearrange("p (b k h) -> p b k h", b=NB, k=NK, h=2)

        def bc(ap):
            return ap.rearrange("p (b h) -> p b h", h=2).unsqueeze(2).to_broadcast([P, NB, NK, 2])

        def by_group(ap):
            return ap.rearrange("p (b k h) -> p b h k", b=NB, k=NK, h=2)

        def groups(ap):
            return ap.rearrange("p (b h) -> p b h", h=2)

        srx = const.tile([P, 64], F32)
        nc.vector.tensor_tensor(out=v4(srx[:]), in0=v4(sr01[:]), in1=bc(sx01[:]), op=ALU.add)
        t1 = const.tile([P, 64], F32)
        nc.vector.scalar_tensor_tensor(out=t1[:], in0=smax[:], scalar=-0.2, in1=srx[:], op0=ALU.mult, op1=ALU.add)
        lg = const.tile([P, 64], F32)
        nc.vector.tensor_scalar(out=lg[:], in0=t1[:], scalar1=-500.0, scalar2=500.0, op0=ALU.max, op1=ALU.min)
        mxk = const.tile([P, 8], F32)
        nc.vector.tensor_reduce(out=groups(mxk[:]), in_=by_group(lg[:]), axis=AX.X, op=ALU.max)
        sh = const.tile([P, 64], F32)
        nc.vector.tensor_tensor(out=v4(sh[:]), in0=v4(lg[:]), in1=bc(mxk[:]), op=ALU.subtract)
        ex = const.tile([P, 64], F32)
        nc.scalar.activation(out=ex[:], in_=sh[:], func=ACT.Exp)
        den = const.tile([P, 8], F32)
        nc.vector.tensor_reduce(out=groups(den[:]), in_=by_group(ex[:]), axis=AX.X, op=ALU.add)
        rden = const.tile([P, 8], F32)
        nc.vector.reciprocal(out=rden[:], in_=den[:])
        nc.vector.tensor_tensor(out=v4(pad[:, 0:64]), in0=v4(ex[:]), in1=bc(rden[:]), op=ALU.mult)
        pt = aux.tile([P, P], F32, name="pt", tag="aux")
        nc.tensor.transpose(pt[:], pad[:], ident_f[:])
        lsum = const.tile([P, 32], F32)
        lg3 = lg[:].rearrange("p (c h) -> p c h", h=2)
        nc.vector.tensor_tensor(out=lsum[:], in0=lg3[:, :, 0], in1=lg3[:, :, 1], op=ALU.add)
        pmean = aux.tile([P, 32], F32, name="pmean", tag="aux")
        nc.tensor.matmul(out=pmean[:], lhsT=ones_f[:], rhs=lsum[:], start=True, stop=True)
        p_out = const.tile([P, P], F32)
        nc.vector.tensor_copy(out=p_out[:], in_=pt[:])
        nc.sync.dma_start(out=out_0.rearrange("b k (h r) w -> (b k h) (r w)", h=2), in_=p_out[0:64, :])
        e_sel = const.tile([P, NB, NK], F32)
        nc.vector.tensor_tensor(
            out=e_sel[:],
            in0=pmean[:].rearrange("p (b k) -> p b k", b=NB),
            in1=ident_f[:, 0:NB].unsqueeze(2).to_broadcast([P, NB, NK]),
            op=ALU.mult,
        )
        e_out = const.tile([P, NK], F32)
        nc.vector.tensor_reduce(out=e_out[:], in_=e_sel[:].rearrange("p b k -> p k b"), axis=AX.X, op=ALU.add)
        nc.sync.dma_start(out=out_1, in_=e_out[0:NB, :])
